import numpy as np
import ml_dtypes


def mxq(x, axis, fmt="e4m3"):
    dtype, down = {"e4m3": (ml_dtypes.float8_e4m3fn, 7), "e5m2": (ml_dtypes.float8_e5m2, 14)}[fmt]
    v = np.moveaxis(np.asarray(x, np.float32).astype(ml_dtypes.bfloat16).astype(np.float64), axis, -1)
    blocks = v.reshape(v.shape[:-1] + (-1, 32))
    amax = np.abs(blocks).max(-1, keepdims=True)
    byte = np.maximum(np.where(amax > 0, np.frexp(amax)[1] - 1 + 127, 0) - down, 1)
    scale = np.exp2(byte - 127.0)
    codes = (blocks / scale).astype(np.float32).astype(dtype).astype(np.float64)
    return np.moveaxis((codes * scale).reshape(v.shape), -1, axis)


WIDE = False


def mx_kscale(k):
    if not WIDE:
        return np.ones(k)
    levels = np.array([10, -10, 5, -5, 0])
    a = np.random.permutation(np.resize(levels, k // 512 * 4)).reshape(k // 512, 4)
    idx = np.arange(k)
    return np.exp2(a[idx // 512, idx % 128 // 32])


BF16 = ml_dtypes.bfloat16


def bf(x):
    return np.asarray(x, np.float32).astype(BF16)


def f64(x):
    return np.asarray(x).astype(np.float64)


N, C, T, V, S, INTER = 2, 512, 16, 128, 3, 128
KT = INTER * T


def setup_inputs():
    s = mx_kscale(C)
    u = mx_kscale(KT)[::T]
    g = np.sqrt(1.5) * KT ** 0.25 / np.sqrt(C)
    mu = 0.25 * np.random.standard_normal((1, C, 1, 1))
    return {'x': bf((np.random.standard_normal((N, C, T, V)) + mu) * s[None, :, None, None]),
            'A': bf(2.0 * np.random.random((S, V, V)) / V),
            'PA': bf(np.random.standard_normal((S, V, V)) / V),
            'Wa': bf(np.random.standard_normal((S, INTER, C)) * g * u[None, :, None] / s[None, None, :]),
            'Wb': bf(np.random.standard_normal((S, INTER, C)) * g / u[None, :, None] / s[None, None, :])}


def reference(x, A, PA, Wa, Wb):
    xq = mxq(f64(x).reshape(N, C, T * V), 1, 'e4m3')
    fa = (mxq(f64(Wa).reshape(S * INTER, C), 1, 'e4m3') @ xq).reshape(N, S, KT, V)
    fb = (mxq(f64(Wb).reshape(S * INTER, C), 1, 'e4m3') @ xq).reshape(N, S, KT, V)
    scores = (np.swapaxes(mxq(fa, 2, 'e4m3'), -1, -2) @ mxq(fb, 2, 'e4m3')) / KT
    e = np.exp(scores - scores.max(-2, keepdims=True))
    attn = e / e.sum(-2, keepdims=True)
    return attn + (f64(A) + f64(PA))[None]

@@ -1,0 +1,263 @@
+from contextlib import ExitStack
+
+import concourse.mybir as mybir
+from concourse.masks import make_identity
+
+F32 = mybir.dt.float32
+BF16 = mybir.dt.bfloat16
+U32 = mybir.dt.uint32
+U8 = mybir.dt.uint8
+FP8X4 = mybir.dt.float8_e4m3fn_x4
+EXP = mybir.ActivationFunctionType.Exp
+
+P = 128
+PACK = 4
+SAMPLES, C, T, V, SUBSETS, INTER = 2, 512, 16, 128, 3, 128
+KT = INTER * T
+GROUPS = T // PACK
+COLS = PACK * V
+HALF = COLS // 2
+AHEAD = 2
+X_AHEAD = 5
+
+FLOPS = 2 * (2 * SUBSETS * INTER) * C * (SAMPLES * T * V) + 2 * SAMPLES * SUBSETS * V * V * KT
+
+
+def tile_unitagcn_pa_kernel(tc, x, A, PA, Wa, Wb, out):
+    nc = tc.nc
+    with ExitStack() as stack:
+        stack.enter_context(tc.manual_schedule())
+        const = stack.enter_context(tc.tile_pool(name="const", bufs=1))
+        w_in = stack.enter_context(tc.tile_pool(name="w_in", bufs=2 * SUBSETS))
+        w_stage = stack.enter_context(tc.tile_pool(name="w_stage", bufs=SUBSETS))
+        x_in = stack.enter_context(tc.tile_pool(name="x_in", bufs=SAMPLES * GROUPS))
+        x_stage = stack.enter_context(tc.tile_pool(name="x_stage", bufs=3))
+        f_stage = stack.enter_context(tc.tile_pool(name="f_stage", bufs=4))
+        f_keep = stack.enter_context(tc.tile_pool(name="f_keep", bufs=SAMPLES))
+        soft = stack.enter_context(tc.tile_pool(name="soft", bufs=4))
+        bank_pool = stack.enter_context(tc.psum_pool(name="bank_pool", bufs=5))
+        joint_pool = stack.enter_context(tc.psum_pool(name="joint_pool", bufs=SUBSETS))
+
+        weights = (Wa, Wb)
+        w_raw = {}
+        x_raw = {}
+        x_rows = x.rearrange("n (p j) t v -> n p j (t v)", j=PACK)
+
+        def load_weights(s):
+            for ab in range(2):
+                raw = w_in.tile([P, C], BF16, name="w_raw")
+                nc.sync.dma_start(out=raw[:], in_=weights[ab][s])
+                w_raw[(ab, s)] = raw
+
+        def load_x(n, g):
+            raw = x_in.tile([P, PACK, COLS], BF16, name="x_raw")
+            nc.sync.dma_start(out=raw[:], in_=x_rows[n, :, :, g * COLS : (g + 1) * COLS])
+            x_raw[(n, g)] = raw
+
+        load_weights(0)
+        load_x(0, 0)
+        load_weights(1)
+        load_weights(2)
+        for n in range(SAMPLES):
+            for g in range(GROUPS):
+                if (n, g) != (0, 0):
+                    load_x(n, g)
+        a_raw = const.tile([P, SUBSETS, V], BF16)
+        nc.sync.dma_start(out=a_raw[:], in_=A.rearrange("s v w -> v s w"))
+        pa_raw = const.tile([P, SUBSETS, V], BF16)
+        nc.sync.dma_start(out=pa_raw[:], in_=PA.rearrange("s v w -> v s w"))
+
+        zero = const.tile([P, 1], F32)
+        nc.vector.memset(zero[:], 0.0)
+        one = const.tile([P, 1], F32)
+        nc.scalar.activation(out=one[:], in_=zero[:], func=EXP)
+
+        ident = const.tile([P, P], F32)
+        make_identity(nc, ident[:])
+        order = const.tile([P, P], F32)
+        for a in range(4):
+            nc.vector.tensor_copy(
+                out=order[:, 32 * a : 32 * a + 32].rearrange("k (c b d) -> k c b d", c=4, b=4, d=2),
+                in_=ident[:, 32 * a : 32 * a + 32].rearrange("k (b c d) -> k c b d", b=4, c=4, d=2),
+            )
+
+        w_codes = const.tile([P, SUBSETS, 2 * INTER], U32, align_bytes=64)
+        w_scales = const.tile([P, SUBSETS, 2 * INTER], U8, align_bytes=64)
+        x_codes = const.tile([P, SAMPLES, T * V], U32, align_bytes=64)
+        x_scales = const.tile([P, SAMPLES, T * V], U8, align_bytes=64)
+        w_grouped = {}
+        x_grouped = {}
+        banks = {}
+        f_grouped = {}
+        f_codes = {}
+        f_scales = {}
+        scores = {}
+        softmax = {}
+
+        def flip_weights(s):
+            flipped = bank_pool.tile([P, 2, 2, INTER], F32, tag="bank")
+            for ab in range(2):
+                halves = w_raw[(ab, s)][:].bitcast(F32).rearrange("i (p u) -> i u p", u=2)
+                for u in range(2):
+                    nc.tensor.transpose(out=flipped[:, ab, u, :], in_=halves[:, u, :], identity=order[:])
+            grouped = w_stage.tile([P, 2, INTER, 2], F32, align_bytes=64, name="w_grouped")
+            nc.scalar.copy(out=grouped[:], in_=flipped[:].rearrange("p ab u i -> p ab i u"))
+            w_grouped[s] = grouped
+
+        def quantise_weights(s):
+            nc.vector.quantize_mx(
+                out=w_codes[:, s, :].bitcast(FP8X4),
+                scales=w_scales[:, s, :],
+                in_=w_grouped[s][:].rearrange("p ab i u -> p (ab i u)").bitcast(BF16),
+            )
+
+        def regroup_x(n, g, half):
+            if half == 0:
+                grouped = x_stage.tile([P, COLS, PACK], BF16, align_bytes=64, name="x_grouped")
+                x_grouped[(n, g)] = grouped
+            cols = slice(half * HALF, (half + 1) * HALF)
+            nc.vector.tensor_copy(
+                out=x_grouped[(n, g)][:, cols, :].rearrange("p (c i) j -> p c j i", i=4),
+                in_=x_raw[(n, g)][:, :, cols].rearrange("p j (c i) -> p c j i", i=4),
+            )
+
+        def quantise_x(n, g):
+            cols = slice(g * COLS, (g + 1) * COLS)
+            nc.vector.quantize_mx(
+                out=x_codes[:, n, cols].bitcast(FP8X4),
+                scales=x_scales[:, n, cols],
+                in_=x_grouped[(n, g)][:].rearrange("p w j -> p (w j)"),
+            )
+
+        def prepare_x(n, g, part):
+            if part < 2:
+                regroup_x(n, g, part)
+            else:
+                quantise_x(n, g)
+
+        def project(n, g, s):
+            cols = slice(g * COLS, (g + 1) * COLS)
+            for ab in range(2):
+                bank = bank_pool.tile([P, COLS], F32, tag="bank")
+                banks[(n, g, s, ab)] = bank
+                nc.tensor.matmul_mx(
+                    out=bank[:],
+                    lhsT=w_codes[:, s, ab * INTER : (ab + 1) * INTER].bitcast(FP8X4),
+                    lhsT_scale=w_scales[:, s, ab * INTER : (ab + 1) * INTER],
+                    rhs=x_codes[:, n, cols].bitcast(FP8X4),
+                    rhs_scale=x_scales[:, n, cols],
+                    start=True,
+                    stop=True,
+                )
+
+        def empty(n, g, s):
+            grouped = f_stage.tile([P, 2, V, PACK], BF16, align_bytes=64, name="f_grouped")
+            f_grouped[(n, g, s)] = grouped
+            for ab in range(2):
+                by_joint = banks[(n, g, s, ab)][:].rearrange("p (j v) -> p v j", j=PACK)
+                if ab == 1 and s == SUBSETS - 1 and g % 2 == 1:
+                    nc.vector.tensor_copy(out=grouped[:, ab, :, :], in_=by_joint)
+                else:
+                    nc.scalar.copy(out=grouped[:, ab, :, :], in_=by_joint)
+
+        def quantise_f(n, g, s):
+            if (g, s) == (0, 0):
+                codes = f_keep.tile([P, GROUPS, SUBSETS, 2 * V], U32, align_bytes=64, name="f_codes")
+                f_codes[n] = codes
+                planes = f_keep.tile([P, GROUPS, SUBSETS, 2 * V], U8, align_bytes=64, name="f_scales")
+                f_scales[n] = planes
+            nc.vector.quantize_mx(
+                out=f_codes[n][:, g, s, :].bitcast(FP8X4),
+                scales=f_scales[n][:, g, s, :],
+                in_=f_grouped[(n, g, s)][:].rearrange("p ab v j -> p (ab v j)"),
+            )
+
+        def score(n, g, s):
+            if g == GROUPS - 1:
+                score_wv = joint_pool.tile([P, V], F32, tag="joint")
+                scores[(n, s)] = score_wv
+                for k in range(GROUPS):
+                    nc.tensor.matmul_mx(
+                        out=score_wv[:],
+                        lhsT=f_codes[n][:, k, s, V : 2 * V].bitcast(FP8X4),
+                        lhsT_scale=f_scales[n][:, k, s, V : 2 * V],
+                        rhs=f_codes[n][:, k, s, 0:V].bitcast(FP8X4),
+                        rhs_scale=f_scales[n][:, k, s, 0:V],
+                        start=(k == 0),
+                        stop=(k == GROUPS - 1),
+                    )
+
+        def find_top(n, g, s):
+            if g == GROUPS - 1:
+                top = soft.tile([P, 1], F32)
+                nc.vector.reduce_max(out=top[:], in_=scores[(n, s)][:], axis=mybir.AxisListType.X)
+                shift = soft.tile([P, 1], F32)
+                nc.vector.tensor_scalar_mul(out=shift[:], in0=top[:], scalar1=-1.0 / KT)
+                softmax[(n, s, "shift")] = shift
+
+        def exponentiate(n, g, s):
+            if g == GROUPS - 1:
+                e = soft.tile([P, V], F32)
+                e_sum = soft.tile([P, 1], F32)
+                nc.scalar.activation(
+                    out=e[:],
+                    in_=scores[(n, s)][:],
+                    func=EXP,
+                    bias=softmax[(n, s, "shift")][:],
+                    scale=1.0 / KT,
+                    accum_out=e_sum[:],
+                )
+                softmax[(n, s, "e")] = e
+                softmax[(n, s, "e_sum")] = e_sum
+
+        def normalise(n, g, s):
+            if g == GROUPS - 1:
+                e_inv = soft.tile([P, 1], F32)
+                nc.vector.reciprocal(out=e_inv[:], in_=softmax[(n, s, "e_sum")][:])
+                attn_wv = soft.tile([P, V], F32)
+                nc.vector.tensor_scalar_mul(out=attn_wv[:], in0=softmax[(n, s, "e")][:], scalar1=e_inv[:])
+                attn_vw = joint_pool.tile([P, V], F32, tag="joint")
+                nc.tensor.transpose(out=attn_vw[:], in_=attn_wv[:], identity=ident[:])
+                softmax[(n, s, "attn_vw")] = attn_vw
+
+        def add_and_store(n, g, s):
+            if g == GROUPS - 1:
+                result = soft.tile([P, V], F32)
+                nc.vector.tensor_tensor(
+                    out=result[:], in0=softmax[(n, s, "attn_vw")][:], in1=adjacency[:, s, :], op=mybir.AluOpType.add
+                )
+                nc.sync.dma_start(out=out[n, s], in_=result[:])
+
+        for s in range(SUBSETS):
+            flip_weights(s)
+        regroup_x(0, 0, 0)
+        regroup_x(0, 0, 1)
+        quantise_weights(0)
+        quantise_x(0, 0)
+        quantise_weights(1)
+        quantise_weights(2)
+        x_parts = [(n, g, part) for n in range(SAMPLES) for g in range(GROUPS) for part in range(3)]
+        for i in range(3, X_AHEAD):
+            prepare_x(*x_parts[i])
+        adjacency = const.tile([P, SUBSETS, V], F32)
+        nc.gpsimd.tensor_tensor(out=adjacency[:], in0=a_raw[:], in1=pa_raw[:], op=mybir.AluOpType.add)
+
+        rounds = [(n, g, s) for n in range(SAMPLES) for g in range(GROUPS) for s in range(SUBSETS)]
+
+        def run(stage, r):
+            if 0 <= r < len(rounds):
+                stage(*rounds[r])
+
+        for r in range(AHEAD):
+            run(project, r)
+        for step in range(len(rounds) + 5):
+            run(empty, step)
+            run(project, step + AHEAD)
+            run(quantise_f, step - 1)
+            run(score, step - 1)
+            if step + X_AHEAD < len(x_parts):
+                prepare_x(*x_parts[step + X_AHEAD])
+            run(find_top, step - 2)
+            run(exponentiate, step - 3)
+            run(normalise, step - 4)
+            run(add_and_store, step - 5)

@@ -54,8 +54,8 @@ def tile_unitagcn_pa_kernel(tc, x, A, PA, Wa, Wb, out):
             nc.sync.dma_start(out=raw[:], in_=x_rows[n, :, :, g * COLS : (g + 1) * COLS])
             x_raw[(n, g)] = raw
 
-        load_weights(0)
         load_x(0, 0)
+        load_weights(0)
         load_weights(1)
         load_weights(2)
         for n in range(SAMPLES):
@@ -189,10 +189,17 @@ def tile_unitagcn_pa_kernel(tc, x, A, PA, Wa, Wb, out):
 
         def find_top(n, g, s):
             if g == GROUPS - 1:
-                top = soft.tile([P, 1], F32)
-                nc.vector.reduce_max(out=top[:], in_=scores[(n, s)][:], axis=mybir.AxisListType.X)
+                negated = soft.tile([P, V], F32)
                 shift = soft.tile([P, 1], F32)
-                nc.vector.tensor_scalar_mul(out=shift[:], in0=top[:], scalar1=-1.0 / KT)
+                nc.vector.tensor_scalar(
+                    out=negated[:],
+                    in0=scores[(n, s)][:],
+                    scalar1=-1.0 / KT,
+                    scalar2=None,
+                    op0=mybir.AluOpType.mult,
+                    op1=mybir.AluOpType.min,
+                    accum_out=shift[:],
+                )
                 softmax[(n, s, "shift")] = shift
 
         def exponentiate(n, g, s):
@@ -232,8 +239,8 @@ def tile_unitagcn_pa_kernel(tc, x, A, PA, Wa, Wb, out):
             flip_weights(s)
         regroup_x(0, 0, 0)
         regroup_x(0, 0, 1)
-        quantise_weights(0)
         quantise_x(0, 0)
+        quantise_weights(0)
         quantise_weights(1)
         quantise_weights(2)
         x_parts = [(n, g, part) for n in range(SAMPLES) for g in range(GROUPS) for part in range(3)]
@@ -250,7 +257,7 @@ def tile_unitagcn_pa_kernel(tc, x, A, PA, Wa, Wb, out):
 
         for r in range(AHEAD):
             run(project, r)
-        for step in range(len(rounds) + 5):
+        for step in range(len(rounds) + 6):
             run(empty, step)
             run(project, step + AHEAD)
             run(quantise_f, step - 1)
@@ -260,4 +267,4 @@ def tile_unitagcn_pa_kernel(tc, x, A, PA, Wa, Wb, out):
             run(find_top, step - 2)
             run(exponentiate, step - 3)
             run(normalise, step - 4)
-            run(add_and_store, step - 5)
+            run(add_and_store, step - 6)

@@ -155,7 +155,9 @@ def tile_unitagcn_pa_kernel(tc, x, A, PA, Wa, Wb, out):
             f_grouped[(n, g, s)] = grouped
             for ab in range(2):
                 by_joint = banks[(n, g, s, ab)][:].rearrange("p (j v) -> p v j", j=PACK)
-                if ab == 1 and s == SUBSETS - 1 and g % 2 == 1:
+                r = rounds.index((n, g, s))
+                period = 4 if r + X_AHEAD < len(x_parts) else 2
+                if ab == 1 and r % period == period - 1:
                     nc.vector.tensor_copy(out=grouped[:, ab, :, :], in_=by_joint)
                 else:
                     nc.scalar.copy(out=grouped[:, ab, :, :], in_=by_joint)

@@ -29,7 +29,7 @@ def tile_unitagcn_pa_kernel(tc, x, A, PA, Wa, Wb, out):
         stack.enter_context(tc.manual_schedule())
         const = stack.enter_context(tc.tile_pool(name="const", bufs=1))
         w_in = stack.enter_context(tc.tile_pool(name="w_in", bufs=2 * SUBSETS))
-        w_stage = stack.enter_context(tc.tile_pool(name="w_stage", bufs=SUBSETS))
+        w_stage = stack.enter_context(tc.tile_pool(name="w_stage", bufs=2 * SUBSETS))
         x_in = stack.enter_context(tc.tile_pool(name="x_in", bufs=SAMPLES * GROUPS))
         x_stage = stack.enter_context(tc.tile_pool(name="x_stage", bufs=3))
         f_stage = stack.enter_context(tc.tile_pool(name="f_stage", bufs=4))
@@ -94,21 +94,21 @@ def tile_unitagcn_pa_kernel(tc, x, A, PA, Wa, Wb, out):
         scores = {}
         softmax = {}
 
-        def flip_weights(s):
-            flipped = bank_pool.tile([P, 2, 2, INTER], F32, tag="bank")
-            for ab in range(2):
-                halves = w_raw[(ab, s)][:].bitcast(F32).rearrange("i (p u) -> i u p", u=2)
-                for u in range(2):
-                    nc.tensor.transpose(out=flipped[:, ab, u, :], in_=halves[:, u, :], identity=order[:])
-            grouped = w_stage.tile([P, 2, INTER, 2], F32, align_bytes=64, name="w_grouped")
-            nc.scalar.copy(out=grouped[:], in_=flipped[:].rearrange("p ab u i -> p ab i u"))
-            w_grouped[s] = grouped
+        def flip_weights(s, ab):
+            flipped = bank_pool.tile([P, 2, INTER], F32, tag="bank")
+            halves = w_raw[(ab, s)][:].bitcast(F32).rearrange("i (p u) -> i u p", u=2)
+            for u in range(2):
+                nc.tensor.transpose(out=flipped[:, u, :], in_=halves[:, u, :], identity=order[:])
+            grouped = w_stage.tile([P, INTER, 2], F32, align_bytes=64, name="w_grouped")
+            nc.scalar.copy(out=grouped[:], in_=flipped[:].rearrange("p u i -> p i u"))
+            w_grouped[(s, ab)] = grouped
 
-        def quantise_weights(s):
+        def quantise_weights(s, ab):
+            cols = slice(ab * INTER, (ab + 1) * INTER)
             nc.vector.quantize_mx(
-                out=w_codes[:, s, :].bitcast(FP8X4),
-                scales=w_scales[:, s, :],
-                in_=w_grouped[s][:].rearrange("p ab i u -> p (ab i u)").bitcast(BF16),
+                out=w_codes[:, s, cols].bitcast(FP8X4),
+                scales=w_scales[:, s, cols],
+                in_=w_grouped[(s, ab)][:].rearrange("p i u -> p (i u)").bitcast(BF16),
             )
 
         def regroup_x(n, g, half):
@@ -155,9 +155,7 @@ def tile_unitagcn_pa_kernel(tc, x, A, PA, Wa, Wb, out):
             f_grouped[(n, g, s)] = grouped
             for ab in range(2):
                 by_joint = banks[(n, g, s, ab)][:].rearrange("p (j v) -> p v j", j=PACK)
-                r = rounds.index((n, g, s))
-                period = 4 if r + X_AHEAD < len(x_parts) else 2
-                if ab == 1 and r % period == period - 1:
+                if ab == 1 and s == SUBSETS - 1 and g % 2 == 1:
                     nc.vector.tensor_copy(out=grouped[:, ab, :, :], in_=by_joint)
                 else:
                     nc.scalar.copy(out=grouped[:, ab, :, :], in_=by_joint)
@@ -238,13 +236,14 @@ def tile_unitagcn_pa_kernel(tc, x, A, PA, Wa, Wb, out):
                 nc.sync.dma_start(out=out[n, s], in_=result[:])
 
         for s in range(SUBSETS):
-            flip_weights(s)
+            for ab in range(2):
+                flip_weights(s, ab)
         regroup_x(0, 0, 0)
         regroup_x(0, 0, 1)
         quantise_x(0, 0)
-        quantise_weights(0)
-        quantise_weights(1)
-        quantise_weights(2)
+        for s in range(SUBSETS):
+            for ab in range(2):
+                quantise_weights(s, ab)
         x_parts = [(n, g, part) for n in range(SAMPLES) for g in range(GROUPS) for part in range(3)]
         for i in range(3, X_AHEAD):
             prepare_x(*x_parts[i])

@@ -18,6 +18,8 @@ GROUPS = T // PACK
 COLS = PACK * V
 HALF = COLS // 2
 AHEAD = 2
+SCALAR_COLS = 160
+VECTOR_BANKS = [(0, 1, 2, 1), (0, 3, 2, 1), (1, 1, 2, 1), (1, 3, 0, 1), (1, 3, 2, 1)]
 X_AHEAD = 5
 
 FLOPS = 2 * (2 * SUBSETS * INTER) * C * (SAMPLES * T * V) + 2 * SAMPLES * SUBSETS * V * V * KT
@@ -117,9 +119,21 @@ def tile_unitagcn_pa_kernel(tc, x, A, PA, Wa, Wb, out):
                 x_grouped[(n, g)] = grouped
             cols = slice(half * HALF, (half + 1) * HALF)
             nc.vector.tensor_copy(
-                out=x_grouped[(n, g)][:, cols, :].rearrange("p (c i) j -> p c j i", i=4),
-                in_=x_raw[(n, g)][:, :, cols].rearrange("p j (c i) -> p c j i", i=4),
+                out=x_grouped[(n, g)][:, cols, :].rearrange("p (c i) j -> p c j i", i=2),
+                in_=x_raw[(n, g)][:, :, cols].rearrange("p j (c i) -> p c j i", i=2),
             )
+
+        def regroup_first_x():
+            grouped = x_stage.tile([P, COLS, PACK], BF16, align_bytes=64, name="x_grouped")
+            x_grouped[(0, 0)] = grouped
+            for engine_copy, cols in (
+                (nc.vector.tensor_copy, slice(0, COLS - SCALAR_COLS)),
+                (nc.scalar.copy, slice(COLS - SCALAR_COLS, COLS)),
+            ):
+                engine_copy(
+                    out=grouped[:, cols, :].rearrange("p (c i) j -> p c j i", i=2),
+                    in_=x_raw[(0, 0)][:, :, cols].rearrange("p j (c i) -> p c j i", i=2),
+                )
 
         def quantise_x(n, g):
             cols = slice(g * COLS, (g + 1) * COLS)
@@ -155,7 +169,7 @@ def tile_unitagcn_pa_kernel(tc, x, A, PA, Wa, Wb, out):
             f_grouped[(n, g, s)] = grouped
             for ab in range(2):
                 by_joint = banks[(n, g, s, ab)][:].rearrange("p (j v) -> p v j", j=PACK)
-                if ab == 1 and s == SUBSETS - 1 and g % 2 == 1:
+                if (n, g, s, ab) in VECTOR_BANKS:
                     nc.vector.tensor_copy(out=grouped[:, ab, :, :], in_=by_joint)
                 else:
                     nc.scalar.copy(out=grouped[:, ab, :, :], in_=by_joint)
@@ -235,11 +249,10 @@ def tile_unitagcn_pa_kernel(tc, x, A, PA, Wa, Wb, out):
                 )
                 nc.sync.dma_start(out=out[n, s], in_=result[:])
 
+        regroup_first_x()
         for s in range(SUBSETS):
             for ab in range(2):
                 flip_weights(s, ab)
-        regroup_x(0, 0, 0)
-        regroup_x(0, 0, 1)
         quantise_x(0, 0)
         for s in range(SUBSETS):
             for ab in range(2):

@@ -231,12 +231,18 @@ def tile_unitagcn_pa_kernel(tc, x, A, PA, Wa, Wb, out):
                 softmax[(n, s, "e")] = e
                 softmax[(n, s, "e_sum")] = e_sum
 
-        def normalise(n, g, s):
+        def invert(n, g, s):
             if g == GROUPS - 1:
                 e_inv = soft.tile([P, 1], F32)
                 nc.vector.reciprocal(out=e_inv[:], in_=softmax[(n, s, "e_sum")][:])
+                softmax[(n, s, "e_inv")] = e_inv
+
+        def normalise(n, g, s):
+            if g == GROUPS - 1:
                 attn_wv = soft.tile([P, V], F32)
-                nc.vector.tensor_scalar_mul(out=attn_wv[:], in0=softmax[(n, s, "e")][:], scalar1=e_inv[:])
+                nc.vector.tensor_scalar_mul(
+                    out=attn_wv[:], in0=softmax[(n, s, "e")][:], scalar1=softmax[(n, s, "e_inv")][:]
+                )
                 attn_vw = joint_pool.tile([P, V], F32, tag="joint")
                 nc.tensor.transpose(out=attn_vw[:], in_=attn_wv[:], identity=ident[:])
                 softmax[(n, s, "attn_vw")] = attn_vw
@@ -254,12 +260,14 @@ def tile_unitagcn_pa_kernel(tc, x, A, PA, Wa, Wb, out):
             for ab in range(2):
                 flip_weights(s, ab)
         quantise_x(0, 0)
-        for s in range(SUBSETS):
+        for s in range(SUBSETS - 1):
             for ab in range(2):
                 quantise_weights(s, ab)
         x_parts = [(n, g, part) for n in range(SAMPLES) for g in range(GROUPS) for part in range(3)]
         for i in range(3, X_AHEAD):
             prepare_x(*x_parts[i])
+        for ab in range(2):
+            quantise_weights(SUBSETS - 1, ab)
         adjacency = const.tile([P, SUBSETS, V], F32)
         nc.gpsimd.tensor_tensor(out=adjacency[:], in0=a_raw[:], in1=pa_raw[:], op=mybir.AluOpType.add)
 
@@ -274,11 +282,12 @@ def tile_unitagcn_pa_kernel(tc, x, A, PA, Wa, Wb, out):
         for step in range(len(rounds) + 6):
             run(empty, step)
             run(project, step + AHEAD)
+            run(invert, step - 4)
             run(quantise_f, step - 1)
             run(score, step - 1)
             if step + X_AHEAD < len(x_parts):
                 prepare_x(*x_parts[step + X_AHEAD])
             run(find_top, step - 2)
             run(exponentiate, step - 3)
-            run(normalise, step - 4)
             run(add_and_store, step - 6)
+            run(normalise, step - 4)

@@ -180,11 +180,14 @@ def tile_unitagcn_pa_kernel(tc, x, A, PA, Wa, Wb, out):
                 f_codes[n] = codes
                 planes = f_keep.tile([P, GROUPS, SUBSETS, 2 * V], U8, align_bytes=64, name="f_scales")
                 f_scales[n] = planes
-            nc.vector.quantize_mx(
-                out=f_codes[n][:, g, s, :].bitcast(FP8X4),
-                scales=f_scales[n][:, g, s, :],
-                in_=f_grouped[(n, g, s)][:].rearrange("p ab v j -> p (ab v j)"),
-            )
+            parts = ((1, 2), (0, 1)) if (n, g, s) == rounds[-1] else ((0, 2),)
+            for first, end in parts:
+                cols = slice(first * V, end * V)
+                nc.vector.quantize_mx(
+                    out=f_codes[n][:, g, s, cols].bitcast(FP8X4),
+                    scales=f_scales[n][:, g, s, cols],
+                    in_=f_grouped[(n, g, s)][:, first:end, :, :].rearrange("p ab v j -> p (ab v j)"),
+                )
 
         def score(n, g, s):
             if g == GROUPS - 1:
@@ -289,5 +292,5 @@ def tile_unitagcn_pa_kernel(tc, x, A, PA, Wa, Wb, out):
                 prepare_x(*x_parts[step + X_AHEAD])
             run(find_top, step - 2)
             run(exponentiate, step - 3)
-            run(add_and_store, step - 6)
             run(normalise, step - 4)
+            run(add_and_store, step - 6)

@@ -16,11 +16,10 @@ SAMPLES, C, T, V, SUBSETS, INTER = 2, 512, 16, 128, 3, 128
 KT = INTER * T
 GROUPS = T // PACK
 COLS = PACK * V
-HALF = COLS // 2
 AHEAD = 2
 SCALAR_COLS = 160
 VECTOR_BANKS = [(0, 1, 2, 1), (0, 3, 2, 1), (1, 1, 2, 1), (1, 3, 0, 1), (1, 3, 2, 1)]
-X_AHEAD = 5
+X_AHEAD = 4
 
 FLOPS = 2 * (2 * SUBSETS * INTER) * C * (SAMPLES * T * V) + 2 * SAMPLES * SUBSETS * V * V * KT
 
@@ -113,14 +112,12 @@ def tile_unitagcn_pa_kernel(tc, x, A, PA, Wa, Wb, out):
                 in_=w_grouped[(s, ab)][:].rearrange("p i u -> p (i u)").bitcast(BF16),
             )
 
-        def regroup_x(n, g, half):
-            if half == 0:
-                grouped = x_stage.tile([P, COLS, PACK], BF16, align_bytes=64, name="x_grouped")
-                x_grouped[(n, g)] = grouped
-            cols = slice(half * HALF, (half + 1) * HALF)
+        def regroup_x(n, g):
+            grouped = x_stage.tile([P, COLS, PACK], BF16, align_bytes=64, name="x_grouped")
+            x_grouped[(n, g)] = grouped
             nc.vector.tensor_copy(
-                out=x_grouped[(n, g)][:, cols, :].rearrange("p (c i) j -> p c j i", i=2),
-                in_=x_raw[(n, g)][:, :, cols].rearrange("p j (c i) -> p c j i", i=2),
+                out=grouped[:].rearrange("p (c i) j -> p c j i", i=2),
+                in_=x_raw[(n, g)][:].rearrange("p j (c i) -> p c j i", i=2),
             )
 
         def regroup_first_x():
@@ -144,9 +141,9 @@ def tile_unitagcn_pa_kernel(tc, x, A, PA, Wa, Wb, out):
             )
 
         def prepare_x(n, g, part):
-            if part < 2:
-                regroup_x(n, g, part)
-            else:
+            if part == 0:
+                regroup_x(n, g)
+            elif part == 1:
                 quantise_x(n, g)
 
         def project(n, g, s):
@@ -267,8 +264,7 @@ def tile_unitagcn_pa_kernel(tc, x, A, PA, Wa, Wb, out):
             for ab in range(2):
                 quantise_weights(s, ab)
         x_parts = [(n, g, part) for n in range(SAMPLES) for g in range(GROUPS) for part in range(3)]
-        for i in range(3, X_AHEAD):
-            prepare_x(*x_parts[i])
+        prepare_x(*x_parts[3])
         for ab in range(2):
             quantise_weights(SUBSETS - 1, ab)
         adjacency = const.tile([P, SUBSETS, V], F32)

@@ -260,13 +260,11 @@ def tile_unitagcn_pa_kernel(tc, x, A, PA, Wa, Wb, out):
             for ab in range(2):
                 flip_weights(s, ab)
         quantise_x(0, 0)
-        for s in range(SUBSETS - 1):
+        for s in range(SUBSETS):
             for ab in range(2):
                 quantise_weights(s, ab)
         x_parts = [(n, g, part) for n in range(SAMPLES) for g in range(GROUPS) for part in range(3)]
         prepare_x(*x_parts[3])
-        for ab in range(2):
-            quantise_weights(SUBSETS - 1, ab)
         adjacency = const.tile([P, SUBSETS, V], F32)
         nc.gpsimd.tensor_tensor(out=adjacency[:], in0=a_raw[:], in1=pa_raw[:], op=mybir.AluOpType.add)
 
@@ -276,17 +274,32 @@ def tile_unitagcn_pa_kernel(tc, x, A, PA, Wa, Wb, out):
             if 0 <= r < len(rounds):
                 stage(*rounds[r])
 
+        lags = {
+            score: (3, 1),
+            find_top: (4, 2),
+            exponentiate: (6, 3),
+            invert: (8, 4),
+            normalise: (8, 4),
+            add_and_store: (10, 6),
+        }
+
+        def run_softmax(stage, step):
+            for n in range(SAMPLES):
+                r = step - lags[stage][n]
+                if 0 <= r < len(rounds) and rounds[r][0] == n:
+                    stage(*rounds[r])
+
         for r in range(AHEAD):
             run(project, r)
         for step in range(len(rounds) + 6):
             run(empty, step)
             run(project, step + AHEAD)
-            run(invert, step - 4)
+            run_softmax(invert, step)
             run(quantise_f, step - 1)
-            run(score, step - 1)
+            run_softmax(score, step)
             if step + X_AHEAD < len(x_parts):
                 prepare_x(*x_parts[step + X_AHEAD])
-            run(find_top, step - 2)
-            run(exponentiate, step - 3)
-            run(normalise, step - 4)
-            run(add_and_store, step - 6)
+            run_softmax(find_top, step)
+            run_softmax(exponentiate, step)
+            run_softmax(normalise, step)
+            run_softmax(add_and_store, step)

@@ -33,7 +33,7 @@ def tile_unitagcn_pa_kernel(tc, x, A, PA, Wa, Wb, out):
         w_stage = stack.enter_context(tc.tile_pool(name="w_stage", bufs=2 * SUBSETS))
         x_in = stack.enter_context(tc.tile_pool(name="x_in", bufs=SAMPLES * GROUPS))
         x_stage = stack.enter_context(tc.tile_pool(name="x_stage", bufs=3))
-        f_stage = stack.enter_context(tc.tile_pool(name="f_stage", bufs=4))
+        f_stage = stack.enter_context(tc.tile_pool(name="f_stage", bufs=5))
         f_keep = stack.enter_context(tc.tile_pool(name="f_keep", bufs=SAMPLES))
         soft = stack.enter_context(tc.tile_pool(name="soft", bufs=4))
         bank_pool = stack.enter_context(tc.psum_pool(name="bank_pool", bufs=5))
@@ -116,8 +116,8 @@ def tile_unitagcn_pa_kernel(tc, x, A, PA, Wa, Wb, out):
             grouped = x_stage.tile([P, COLS, PACK], BF16, align_bytes=64, name="x_grouped")
             x_grouped[(n, g)] = grouped
             nc.vector.tensor_copy(
-                out=grouped[:].rearrange("p (c i) j -> p c j i", i=2),
-                in_=x_raw[(n, g)][:].rearrange("p j (c i) -> p c j i", i=2),
+                out=grouped[:].rearrange("p (c i) j -> p c j i", i=4),
+                in_=x_raw[(n, g)][:].rearrange("p j (c i) -> p c j i", i=4),
             )
 
         def regroup_first_x():
@@ -128,8 +128,8 @@ def tile_unitagcn_pa_kernel(tc, x, A, PA, Wa, Wb, out):
                 (nc.scalar.copy, slice(COLS - SCALAR_COLS, COLS)),
             ):
                 engine_copy(
-                    out=grouped[:, cols, :].rearrange("p (c i) j -> p c j i", i=2),
-                    in_=x_raw[(0, 0)][:, :, cols].rearrange("p j (c i) -> p c j i", i=2),
+                    out=grouped[:, cols, :].rearrange("p (c i) j -> p c j i", i=4),
+                    in_=x_raw[(0, 0)][:, :, cols].rearrange("p j (c i) -> p c j i", i=4),
                 )
 
         def quantise_x(n, g):
@@ -283,6 +283,16 @@ def tile_unitagcn_pa_kernel(tc, x, A, PA, Wa, Wb, out):
             add_and_store: (10, 6),
         }
 
+        def run_quantise(step):
+            r = step - 2
+            if r < len(rounds) - 4:
+                run(quantise_f, r)
+            elif r == len(rounds) - 4:
+                for i in range(r, r + 2):
+                    run(quantise_f, i)
+            else:
+                run(quantise_f, step - 1)
+
         def run_softmax(stage, step):
             for n in range(SAMPLES):
                 r = step - lags[stage][n]
@@ -295,7 +305,7 @@ def tile_unitagcn_pa_kernel(tc, x, A, PA, Wa, Wb, out):
             run(empty, step)
             run(project, step + AHEAD)
             run_softmax(invert, step)
-            run(quantise_f, step - 1)
+            run_quantise(step)
             run_softmax(score, step)
             if step + X_AHEAD < len(x_parts):
                 prepare_x(*x_parts[step + X_AHEAD])

from contextlib import ExitStack

import concourse.mybir as mybir
from concourse.masks import make_identity

F32 = mybir.dt.float32
BF16 = mybir.dt.bfloat16
U32 = mybir.dt.uint32
U8 = mybir.dt.uint8
FP8X4 = mybir.dt.float8_e4m3fn_x4
EXP = mybir.ActivationFunctionType.Exp

P = 128
PACK = 4
SAMPLES, C, T, V, SUBSETS, INTER = 2, 512, 16, 128, 3, 128
KT = INTER * T
GROUPS = T // PACK
COLS = PACK * V
AHEAD = 2
SCALAR_COLS = 160
VECTOR_BANKS = [(0, 1, 2, 1), (0, 3, 2, 1), (1, 1, 2, 1), (1, 3, 0, 1), (1, 3, 2, 1)]
X_AHEAD = 4

FLOPS = 2 * (2 * SUBSETS * INTER) * C * (SAMPLES * T * V) + 2 * SAMPLES * SUBSETS * V * V * KT


def tile_unitagcn_pa_kernel(tc, x, A, PA, Wa, Wb, out):
    nc = tc.nc
    with ExitStack() as stack:
        stack.enter_context(tc.manual_schedule())
        const = stack.enter_context(tc.tile_pool(name="const", bufs=1))
        w_in = stack.enter_context(tc.tile_pool(name="w_in", bufs=2 * SUBSETS))
        w_stage = stack.enter_context(tc.tile_pool(name="w_stage", bufs=2 * SUBSETS))
        x_in = stack.enter_context(tc.tile_pool(name="x_in", bufs=SAMPLES * GROUPS))
        x_stage = stack.enter_context(tc.tile_pool(name="x_stage", bufs=3))
        f_stage = stack.enter_context(tc.tile_pool(name="f_stage", bufs=5))
        f_keep = stack.enter_context(tc.tile_pool(name="f_keep", bufs=SAMPLES))
        soft = stack.enter_context(tc.tile_pool(name="soft", bufs=4))
        bank_pool = stack.enter_context(tc.psum_pool(name="bank_pool", bufs=5))
        joint_pool = stack.enter_context(tc.psum_pool(name="joint_pool", bufs=SUBSETS))

        weights = (Wa, Wb)
        w_raw = {}
        x_raw = {}
        x_rows = x.rearrange("n (p j) t v -> n p j (t v)", j=PACK)

        def load_weights(s):
            for ab in range(2):
                raw = w_in.tile([P, C], BF16, name="w_raw")
                nc.sync.dma_start(out=raw[:], in_=weights[ab][s])
                w_raw[(ab, s)] = raw

        def load_x(n, g):
            raw = x_in.tile([P, PACK, COLS], BF16, name="x_raw")
            nc.sync.dma_start(out=raw[:], in_=x_rows[n, :, :, g * COLS : (g + 1) * COLS])
            x_raw[(n, g)] = raw

        load_x(0, 0)
        load_weights(0)
        load_weights(1)
        load_weights(2)
        for n in range(SAMPLES):
            for g in range(GROUPS):
                if (n, g) != (0, 0):
                    load_x(n, g)
        a_raw = const.tile([P, SUBSETS, V], BF16)
        nc.sync.dma_start(out=a_raw[:], in_=A.rearrange("s v w -> v s w"))
        pa_raw = const.tile([P, SUBSETS, V], BF16)
        nc.sync.dma_start(out=pa_raw[:], in_=PA.rearrange("s v w -> v s w"))

        zero = const.tile([P, 1], F32)
        nc.vector.memset(zero[:], 0.0)
        one = const.tile([P, 1], F32)
        nc.scalar.activation(out=one[:], in_=zero[:], func=EXP)

        ident = const.tile([P, P], F32)
        make_identity(nc, ident[:])
        order = const.tile([P, P], F32)
        for a in range(4):
            nc.vector.tensor_copy(
                out=order[:, 32 * a : 32 * a + 32].rearrange("k (c b d) -> k c b d", c=4, b=4, d=2),
                in_=ident[:, 32 * a : 32 * a + 32].rearrange("k (b c d) -> k c b d", b=4, c=4, d=2),
            )

        w_codes = const.tile([P, SUBSETS, 2 * INTER], U32, align_bytes=64)
        w_scales = const.tile([P, SUBSETS, 2 * INTER], U8, align_bytes=64)
        x_codes = const.tile([P, SAMPLES, T * V], U32, align_bytes=64)
        x_scales = const.tile([P, SAMPLES, T * V], U8, align_bytes=64)
        w_grouped = {}
        x_grouped = {}
        banks = {}
        f_grouped = {}
        f_codes = {}
        f_scales = {}
        scores = {}
        softmax = {}

        def flip_weights(s, ab):
            flipped = bank_pool.tile([P, 2, INTER], F32, tag="bank")
            halves = w_raw[(ab, s)][:].bitcast(F32).rearrange("i (p u) -> i u p", u=2)
            for u in range(2):
                nc.tensor.transpose(out=flipped[:, u, :], in_=halves[:, u, :], identity=order[:])
            grouped = w_stage.tile([P, INTER, 2], F32, align_bytes=64, name="w_grouped")
            nc.scalar.copy(out=grouped[:], in_=flipped[:].rearrange("p u i -> p i u"))
            w_grouped[(s, ab)] = grouped

        def quantise_weights(s, ab):
            cols = slice(ab * INTER, (ab + 1) * INTER)
            nc.vector.quantize_mx(
                out=w_codes[:, s, cols].bitcast(FP8X4),
                scales=w_scales[:, s, cols],
                in_=w_grouped[(s, ab)][:].rearrange("p i u -> p (i u)").bitcast(BF16),
            )

        def regroup_x(n, g):
            grouped = x_stage.tile([P, COLS, PACK], BF16, align_bytes=64, name="x_grouped")
            x_grouped[(n, g)] = grouped
            nc.vector.tensor_copy(
                out=grouped[:].rearrange("p (c i) j -> p c j i", i=4),
                in_=x_raw[(n, g)][:].rearrange("p j (c i) -> p c j i", i=4),
            )

        def regroup_first_x():
            grouped = x_stage.tile([P, COLS, PACK], BF16, align_bytes=64, name="x_grouped")
            x_grouped[(0, 0)] = grouped
            for engine_copy, cols in (
                (nc.vector.tensor_copy, slice(0, COLS - SCALAR_COLS)),
                (nc.scalar.copy, slice(COLS - SCALAR_COLS, COLS)),
            ):
                engine_copy(
                    out=grouped[:, cols, :].rearrange("p (c i) j -> p c j i", i=4),
                    in_=x_raw[(0, 0)][:, :, cols].rearrange("p j (c i) -> p c j i", i=4),
                )

        def quantise_x(n, g):
            cols = slice(g * COLS, (g + 1) * COLS)
            nc.vector.quantize_mx(
                out=x_codes[:, n, cols].bitcast(FP8X4),
                scales=x_scales[:, n, cols],
                in_=x_grouped[(n, g)][:].rearrange("p w j -> p (w j)"),
            )

        def prepare_x(n, g, part):
            if part == 0:
                regroup_x(n, g)
            elif part == 1:
                quantise_x(n, g)

        def project(n, g, s):
            cols = slice(g * COLS, (g + 1) * COLS)
            for ab in range(2):
                bank = bank_pool.tile([P, COLS], F32, tag="bank")
                banks[(n, g, s, ab)] = bank
                nc.tensor.matmul_mx(
                    out=bank[:],
                    lhsT=w_codes[:, s, ab * INTER : (ab + 1) * INTER].bitcast(FP8X4),
                    lhsT_scale=w_scales[:, s, ab * INTER : (ab + 1) * INTER],
                    rhs=x_codes[:, n, cols].bitcast(FP8X4),
                    rhs_scale=x_scales[:, n, cols],
                    start=True,
                    stop=True,
                )

        def empty(n, g, s):
            grouped = f_stage.tile([P, 2, V, PACK], BF16, align_bytes=64, name="f_grouped")
            f_grouped[(n, g, s)] = grouped
            for ab in range(2):
                by_joint = banks[(n, g, s, ab)][:].rearrange("p (j v) -> p v j", j=PACK)
                if (n, g, s, ab) in VECTOR_BANKS:
                    nc.vector.tensor_copy(out=grouped[:, ab, :, :], in_=by_joint)
                else:
                    nc.scalar.copy(out=grouped[:, ab, :, :], in_=by_joint)

        def quantise_f(n, g, s):
            if (g, s) == (0, 0):
                codes = f_keep.tile([P, GROUPS, SUBSETS, 2 * V], U32, align_bytes=64, name="f_codes")
                f_codes[n] = codes
                planes = f_keep.tile([P, GROUPS, SUBSETS, 2 * V], U8, align_bytes=64, name="f_scales")
                f_scales[n] = planes
            parts = ((1, 2), (0, 1)) if (n, g, s) == rounds[-1] else ((0, 2),)
            for first, end in parts:
                cols = slice(first * V, end * V)
                nc.vector.quantize_mx(
                    out=f_codes[n][:, g, s, cols].bitcast(FP8X4),
                    scales=f_scales[n][:, g, s, cols],
                    in_=f_grouped[(n, g, s)][:, first:end, :, :].rearrange("p ab v j -> p (ab v j)"),
                )

        def score(n, g, s):
            if g == GROUPS - 1:
                score_wv = joint_pool.tile([P, V], F32, tag="joint")
                scores[(n, s)] = score_wv
                for k in range(GROUPS):
                    nc.tensor.matmul_mx(
                        out=score_wv[:],
                        lhsT=f_codes[n][:, k, s, V : 2 * V].bitcast(FP8X4),
                        lhsT_scale=f_scales[n][:, k, s, V : 2 * V],
                        rhs=f_codes[n][:, k, s, 0:V].bitcast(FP8X4),
                        rhs_scale=f_scales[n][:, k, s, 0:V],
                        start=(k == 0),
                        stop=(k == GROUPS - 1),
                    )

        def find_top(n, g, s):
            if g == GROUPS - 1:
                negated = soft.tile([P, V], F32)
                shift = soft.tile([P, 1], F32)
                nc.vector.tensor_scalar(
                    out=negated[:],
                    in0=scores[(n, s)][:],
                    scalar1=-1.0 / KT,
                    scalar2=None,
                    op0=mybir.AluOpType.mult,
                    op1=mybir.AluOpType.min,
                    accum_out=shift[:],
                )
                softmax[(n, s, "shift")] = shift

        def exponentiate(n, g, s):
            if g == GROUPS - 1:
                e = soft.tile([P, V], F32)
                e_sum = soft.tile([P, 1], F32)
                nc.scalar.activation(
                    out=e[:],
                    in_=scores[(n, s)][:],
                    func=EXP,
                    bias=softmax[(n, s, "shift")][:],
                    scale=1.0 / KT,
                    accum_out=e_sum[:],
                )
                softmax[(n, s, "e")] = e
                softmax[(n, s, "e_sum")] = e_sum

        def invert(n, g, s):
            if g == GROUPS - 1:
                e_inv = soft.tile([P, 1], F32)
                nc.vector.reciprocal(out=e_inv[:], in_=softmax[(n, s, "e_sum")][:])
                softmax[(n, s, "e_inv")] = e_inv

        def normalise(n, g, s):
            if g == GROUPS - 1:
                attn_wv = soft.tile([P, V], F32)
                nc.vector.tensor_scalar_mul(
                    out=attn_wv[:], in0=softmax[(n, s, "e")][:], scalar1=softmax[(n, s, "e_inv")][:]
                )
                attn_vw = joint_pool.tile([P, V], F32, tag="joint")
                nc.tensor.transpose(out=attn_vw[:], in_=attn_wv[:], identity=ident[:])
                softmax[(n, s, "attn_vw")] = attn_vw

        def add_and_store(n, g, s):
            if g == GROUPS - 1:
                result = soft.tile([P, V], F32)
                nc.vector.tensor_tensor(
                    out=result[:], in0=softmax[(n, s, "attn_vw")][:], in1=adjacency[:, s, :], op=mybir.AluOpType.add
                )
                nc.sync.dma_start(out=out[n, s], in_=result[:])

        regroup_first_x()
        for s in range(SUBSETS):
            for ab in range(2):
                flip_weights(s, ab)
        quantise_x(0, 0)
        for s in range(SUBSETS):
            for ab in range(2):
                quantise_weights(s, ab)
        x_parts = [(n, g, part) for n in range(SAMPLES) for g in range(GROUPS) for part in range(3)]
        prepare_x(*x_parts[3])
        adjacency = const.tile([P, SUBSETS, V], F32)
        nc.gpsimd.tensor_tensor(out=adjacency[:], in0=a_raw[:], in1=pa_raw[:], op=mybir.AluOpType.add)

        rounds = [(n, g, s) for n in range(SAMPLES) for g in range(GROUPS) for s in range(SUBSETS)]

        def run(stage, r):
            if 0 <= r < len(rounds):
                stage(*rounds[r])

        lags = {
            score: (3, 1),
            find_top: (4, 2),
            exponentiate: (6, 3),
            invert: (8, 4),
            normalise: (8, 4),
            add_and_store: (10, 6),
        }

        def run_quantise(step):
            r = step - 2
            if r < len(rounds) - 4:
                run(quantise_f, r)
            elif r == len(rounds) - 4:
                for i in range(r, r + 2):
                    run(quantise_f, i)
            else:
                run(quantise_f, step - 1)

        def run_softmax(stage, step):
            for n in range(SAMPLES):
                r = step - lags[stage][n]
                if 0 <= r < len(rounds) and rounds[r][0] == n:
                    stage(*rounds[r])

        for r in range(AHEAD):
            run(project, r)
        for step in range(len(rounds) + 6):
            run(empty, step)
            run(project, step + AHEAD)
            run_softmax(invert, step)
            run_quantise(step)
            run_softmax(score, step)
            if step + X_AHEAD < len(x_parts):
                prepare_x(*x_parts[step + X_AHEAD])
            run_softmax(find_top, step)
            run_softmax(exponentiate, step)
            run_softmax(normalise, step)
            run_softmax(add_and_store, step)
